import numpy as np
import ml_dtypes


def mxq(x, axis, fmt="e4m3"):
    dtype, down = {"e4m3": (ml_dtypes.float8_e4m3fn, 7), "e5m2": (ml_dtypes.float8_e5m2, 14)}[fmt]
    v = np.moveaxis(np.asarray(x, np.float32).astype(ml_dtypes.bfloat16).astype(np.float64), axis, -1)
    blocks = v.reshape(v.shape[:-1] + (-1, 32))
    amax = np.abs(blocks).max(-1, keepdims=True)
    byte = np.maximum(np.where(amax > 0, np.frexp(amax)[1] - 1 + 127, 0) - down, 1)
    scale = np.exp2(byte - 127.0)
    codes = (blocks / scale).astype(np.float32).astype(dtype).astype(np.float64)
    return np.moveaxis((codes * scale).reshape(v.shape), -1, axis)


WIDE = False


def mx_kscale(k):
    if not WIDE:
        return np.ones(k)
    levels = np.array([18, -18])
    if k % 512:
        return np.exp2(np.random.permutation(np.resize(levels, k // 32))).repeat(32)
    a = np.empty((k // 512, 16))
    for p in range(k // 512):
        a[p, :8] = np.random.permutation(np.resize(levels, 8))
        for g in range(8):
            far = levels[np.abs(levels - a[p, g]) >= 10]
            a[p, g + 8] = far[np.random.randint(len(far))]
    return np.exp2(a.ravel()).repeat(32)


BF16 = ml_dtypes.bfloat16


def bf(x):
    return np.asarray(x, np.float32).astype(BF16)


def f64(x):
    return np.asarray(x).astype(np.float64)


N, CIN, COUT, V, T, S = 1, 512, 128, 32, 1, 16
EPS = 1e-5
KG = S * V


def pre_relu(ada_A, ada_w, ada_b, PA, feat, bn_gamma, bn_beta, bn_mean, bn_var, res):
    adaA = (f64(ada_w).reshape(S * COUT, CIN) @ f64(ada_A).reshape(N, CIN, V * V)).reshape(N, S, COUT, V, V)
    adaA = adaA.transpose(1, 0, 2, 3, 4) + f64(ada_b)[:, None, :, None, None]
    A_full = adaA * f64(PA)[:, None, None, :, :]
    Ag = A_full.transpose(1, 2, 3, 0, 4).reshape(N, COUT, V, KG)
    Fg = f64(feat).transpose(1, 2, 0, 3, 4).reshape(N, COUT, KG, T)
    y = Ag @ Fg
    scale = f64(bn_gamma) / np.sqrt(f64(bn_var) + EPS)
    z = (y - f64(bn_mean)[:, None, None]) * scale[:, None, None] + f64(bn_beta)[:, None, None]
    return z + f64(res)


def setup_inputs():
    r = np.random.standard_normal
    sv = mx_kscale(V * V).reshape(V, V)[:, 0]
    u = mx_kscale(S * COUT).reshape(S, COUT)
    ada_A0 = bf(r((N, CIN, V, V)))
    ada_w0 = bf(r((S, COUT, CIN)) / np.sqrt(CIN))
    ada_b = bf(r((S, COUT)) * 0.3)
    PA = bf(r((S, V, V)) * 2.0 / np.sqrt(KG))
    feat0 = bf(r((S, N, COUT, V, T)))
    bn_gamma = bf(1.0 + 0.1 * r(COUT))
    bn_beta = bf(0.3 * r(COUT))
    bn_mean = bf(0.3 * r(COUT))
    bn_var = bf(np.abs(r(COUT)) + 1.0)
    res = bf(r((N, COUT, V, T)) * 0.9)
    g = bf(16.0 * r((N, COUT, V, T)) * np.exp2(np.random.randint(-6, 1, (N, 1, V, T))) / sv[None, None, :, None])
    h = pre_relu(ada_A0, ada_w0, ada_b, PA, feat0, bn_gamma, bn_beta, bn_mean, bn_var, res)
    return {"ada_A": bf(f64(ada_A0) * sv[None, None, :, None]),
            "ada_w": bf(f64(ada_w0) / u[:, :, None]),
            "ada_b": ada_b,
            "PA": PA,
            "feat": bf(f64(feat0) * u[:, None, :, None, None]),
            "bn_gamma": bn_gamma,
            "bn_beta": bn_beta,
            "bn_mean": bn_mean,
            "bn_var": bn_var,
            "res": res,
            "h": np.asarray(h, np.float32),
            "grad_out": g}


def reference(ada_A, ada_w, ada_b, PA, feat, bn_gamma, bn_beta, bn_mean, bn_var, res, h, grad_out):
    scale = f64(bn_gamma) / np.sqrt(f64(bn_var) + EPS)
    dy = (np.where(f64(h) > 0.0, f64(grad_out), 0.0) * scale[:, None, None])[0, :, :, 0]
    f1 = f64(feat)[:, 0, :, :, 0]
    dz = dy[None, :, :, None] * f1[:, :, None, :] * f64(PA)[:, None, :, :]
    dz = dz.reshape(S * COUT, V * V)
    wq = mxq(f64(ada_w).reshape(S * COUT, CIN), 0, "e4m3")
    aq = mxq(f64(ada_A).reshape(CIN, V * V), 1, "e4m3")
    da = wq.T @ mxq(dz, 0, "e5m2")
    dw = mxq(dz, 1, "e5m2") @ aq.T
    return da.reshape(N, CIN, V, V), dw.reshape(S, COUT, CIN)

@@ -1,0 +1,315 @@
+from contextlib import ExitStack
+
+import concourse.mybir as mybir
+from concourse.masks import make_identity
+
+F32 = mybir.dt.float32
+BF16 = mybir.dt.bfloat16
+U32 = mybir.dt.uint32
+U8 = mybir.dt.uint8
+E4M3 = mybir.dt.float8_e4m3fn_x4
+E5M2 = mybir.dt.float8_e5m2_x4
+ALU = mybir.AluOpType
+ACT = mybir.ActivationFunctionType
+
+CIN, COUT, V, S = 512, 128, 32, 16
+EPS = 1e-5
+P = 128
+PACK = 4
+N_TILE = 512
+HALF_V = 16
+
+FLOPS = 2 * 2 * (S * COUT) * CIN * (V * V)
+BYTES = 2 * (CIN * V * V + S * COUT * CIN + S * V * V + S * COUT * V + 2 * COUT + COUT * V) + 4 * (
+    COUT * V + CIN * V * V + S * COUT * CIN
+)
+
+
+def tile_multiscale_gcn_pa_v_kernel(
+    tc, ada_A, ada_w, ada_b, PA, feat, bn_gamma, bn_beta, bn_mean, bn_var, res, h, grad_out, out_0, out_1
+):
+    nc = tc.nc
+    with ExitStack() as ctx:
+        keep = ctx.enter_context(tc.tile_pool(name="keep", bufs=1))
+        outs = ctx.enter_context(tc.tile_pool(name="outs", bufs=8))
+        psum_f = ctx.enter_context(tc.psum_pool(name="psum_f", bufs=1))
+        psum = ctx.enter_context(tc.psum_pool(name="psum", bufs=7))
+        ctx.enter_context(tc.manual_schedule())
+
+        var_sb = keep.tile([P, PACK], BF16, name="var_sb")
+        gamma_sb = keep.tile([P, PACK], BF16, name="gamma_sb")
+        h_sb = keep.tile([P, PACK * V], F32, name="h_sb")
+        g_sb = keep.tile([P, PACK * V], BF16, name="g_sb")
+        f_sb = keep.tile([P, 4 * PACK * V], BF16, name="f_sb")
+        pa_sb = [keep.tile([P, 4 * N_TILE], BF16, name="pa_sb%d" % i) for i in range(2)]
+        w_sb = [keep.tile([P, PACK * CIN], BF16, name="w_sb%d" % i) for i in range(4)]
+        a_sb = [keep.tile([P, 4 * N_TILE], BF16, name="a_sb%d" % i) for i in range(2)]
+        dz = [keep.tile([P, PACK * 4 * N_TILE], BF16, name="dz%d" % i) for i in range(2)]
+        ident = keep.tile([P, P], F32, name="ident")
+
+        pa_view = PA.rearrange("(g a) (x v) w -> a x g (v w)", a=4, x=2)
+        w_view = ada_w.rearrange("(g a) (c t) i -> g (a c) (t i)", a=4, t=PACK)
+        a_view = ada_A.rearrange("n (b p) (x v) w -> x p (n b) (v w)", p=P, x=2)
+        out0_view = out_0.rearrange("n (b p) (x v) w -> x (n b) p (v w)", p=P, x=2)
+        out1_view = out_1.rearrange("(g a) (c t) i -> t g (a c) i", a=4, t=PACK)
+
+        def load_pa(queue, half):
+            for a in range(4):
+                queue.dma_start(
+                    out=pa_sb[half][32 * a : 32 * (a + 1), :].rearrange("p (g c) -> p g c", g=4),
+                    in_=pa_view[a, half].partition_broadcast(32),
+                )
+
+        nc.sync.dma_start(out=var_sb[:], in_=bn_var.rearrange("(c t) -> c t", t=PACK).partition_broadcast(4))
+        nc.sync.dma_start(
+            out=f_sb[:].rearrange("p (g c) -> p g c", g=4),
+            in_=feat.rearrange("(g a) n (c t) w x -> (a c) g (t w n x)", a=4, t=PACK),
+        )
+        nc.sync.dma_start(
+            out=h_sb[:], in_=h.rearrange("n (c t) v x -> c (t v n x)", t=PACK).partition_broadcast(4)
+        )
+        nc.sync.dma_start(
+            out=g_sb[:], in_=grad_out.rearrange("n (c t) v x -> c (t v n x)", t=PACK).partition_broadcast(4)
+        )
+        nc.gpsimd.dma_start(out=gamma_sb[:], in_=bn_gamma.rearrange("(c t) -> c t", t=PACK).partition_broadcast(4))
+        load_pa(nc.scalar, 0)
+        make_identity(nc, ident[:])
+
+        def load_w(g):
+            nc.sync.dma_start(out=w_sb[g][:], in_=w_view[g])
+
+        def load_a(half):
+            nc.sync.dma_start(out=a_sb[half][:].rearrange("p (b c) -> p b c", b=4), in_=a_view[half])
+
+        load_w(0)
+        load_w(1)
+        load_a(0)
+        load_w(2)
+        load_a(1)
+        load_w(3)
+        load_pa(nc.sync, 1)
+
+        std = keep.tile([P, PACK], F32, name="std")
+        rstd = keep.tile([P, PACK], F32, name="rstd")
+        masked = keep.tile([P, PACK * V], F32, name="masked")
+        gained = keep.tile([P, PACK * V], F32, name="gained")
+        dy = keep.tile([P, PACK * V], F32, name="dy")
+        nc.scalar.activation(out=std[:], in_=var_sb[:], func=ACT.Sqrt, bias=EPS)
+
+        f_turned_ps = psum.tile([P, N_TILE], F32, name="bank")
+        f_turned = keep.tile([P, 2 * P], F32, name="f_turned")
+        f_ps = psum_f.tile([P, N_TILE], F32, name="f_ps")
+        for b in range(2):
+            cols = slice(b * P, (b + 1) * P)
+            nc.tensor.transpose(f_turned_ps[:, cols], f_sb[:].bitcast(F32)[:, cols], ident[:])
+        nc.scalar.copy(out=f_turned[:], in_=f_turned_ps[:, : 2 * P])
+        for b in range(2):
+            cols = slice(b * P, (b + 1) * P)
+            nc.tensor.transpose(f_ps[:, cols], f_turned[:, cols], ident[:])
+        f_gtw = f_ps[:, : 2 * P].bitcast(BF16).rearrange("p (g t w) -> p g t w", g=4, t=PACK)
+
+        def by_tv(ap):
+            return ap.rearrange("p (t v) -> p t v", t=PACK)
+
+        def over_v(ap):
+            return ap.unsqueeze(2).to_broadcast([P, PACK, V])
+
+        nc.vector.scalar_tensor_tensor(
+            out=masked[:], in0=h_sb[:], scalar=0.0, in1=g_sb[:], op0=ALU.is_gt, op1=ALU.mult
+        )
+        nc.vector.reciprocal(out=rstd[:], in_=std[:])
+        nc.vector.tensor_tensor(out=by_tv(gained[:]), in0=by_tv(masked[:]), in1=over_v(gamma_sb[:]), op=ALU.mult)
+        nc.vector.tensor_tensor(out=by_tv(dy[:]), in0=by_tv(gained[:]), in1=over_v(rstd[:]), op=ALU.mult)
+
+        grouped = {}
+        codes = {}
+        scales = {}
+
+        def new_grouped(key, tag=None):
+            grouped[key] = keep.tile(
+                [P, PACK * N_TILE], BF16, name="grouped_%s%d%d" % key, tag=tag or ("grouped_%s%d%d" % key),
+                align_bytes=64,
+            )
+            return grouped[key]
+
+        def dz_row(half, t):
+            dz_view = dz[half][:].rearrange("p (t g v w) -> p t g v w", t=PACK, g=4, v=HALF_V)
+            pa_gvw = pa_sb[half][:].rearrange("p (g v w) -> p g v w", g=4, v=HALF_V)
+            for v in range(HALF_V):
+                col = t * V + half * HALF_V + v
+                nc.vector.scalar_tensor_tensor(
+                    out=dz_view[:, t, :, v, :],
+                    in0=f_gtw[:, :, t, :],
+                    scalar=dy[:, col : col + 1],
+                    in1=pa_gvw[:, :, v, :],
+                    op0=ALU.mult,
+                    op1=ALU.mult,
+                )
+
+        banks = {}
+
+        def turn(key, words):
+            for j in range(2):
+                bank = psum.tile([P, N_TILE], F32, name="bank")
+                banks[key + (j,)] = bank
+                for a in range(2):
+                    for u in range(2):
+                        base = (2 * j + a) * 2 * P
+                        slot = (2 * a + u) * P
+                        nc.tensor.transpose(
+                            bank[:, slot : slot + P], words[:, base + u : base + 2 * P : 2], ident[:]
+                        )
+
+        def turn_dz(half, t):
+            turn(("d", half, t), dz[half][:].bitcast(F32)[:, t * 2 * N_TILE : (t + 1) * 2 * N_TILE])
+
+        def turn_a(half):
+            turn(("a", half, 0), a_sb[half][:].bitcast(F32))
+
+        def turned_out(key):
+            dst = new_grouped(key)[:].bitcast(F32).rearrange("p (j a r u) -> p j a r u", j=2, a=2, u=2)
+            for j in range(2):
+                src = banks[key + (j,)][:].rearrange("p (a u r) -> p a r u", a=2, u=2)
+                nc.scalar.copy(out=dst[:, j], in_=src)
+
+        def interleave(engine, key, rows, tag=None):
+            tile = new_grouped(key, tag)
+            if engine == "pool":
+                for j in range(2):
+                    cols = slice(j * N_TILE // 2, (j + 1) * N_TILE // 2)
+                    nc.gpsimd.tensor_scalar(
+                        out=tile[:].rearrange("p (c t) -> p c t", t=PACK)[:, cols, :],
+                        in0=rows.rearrange("p t c -> p c t")[:, cols, :],
+                        scalar1=1.0,
+                        scalar2=0.0,
+                        op0=ALU.mult,
+                        op1=ALU.add,
+                    )
+                return
+            dst = tile[:].rearrange("p (c i t) -> p c t i", i=4, t=PACK)
+            src = rows.rearrange("p t (c i) -> p c t i", i=4)
+            if engine == "act":
+                nc.scalar.copy(out=dst, in_=src)
+            else:
+                nc.vector.tensor_copy(out=dst, in_=src)
+
+        def inter_w(engine, g):
+            interleave(engine, ("w", g, 0), w_sb[g][:].rearrange("p (t c) -> p t c", t=PACK))
+
+        def inter_dz(engine, half, g, tag=None):
+            rows = dz[half][:].rearrange("p (t g c) -> p g t c", t=PACK, g=4)[:, g]
+            interleave(engine, ("z", half, g), rows, tag)
+
+        def quant(key):
+            fmt = E4M3 if key[0] in "wa" else E5M2
+            codes[key] = keep.tile([P, N_TILE], U32, name="codes_%s%d%d" % key, align_bytes=64)
+            scales[key] = keep.tile([P, N_TILE], U8, name="scales_%s%d%d" % key, align_bytes=64)
+            nc.vector.quantize_mx(out=codes[key][:].bitcast(fmt), scales=scales[key][:], in_=grouped[key][:])
+
+        def mx_pass(bank, stat, stat_fmt, block, mov, mov_fmt, start, stop):
+            cols = slice(block * P, (block + 1) * P)
+            nc.tensor.matmul_mx(
+                out=bank[:],
+                lhsT=codes[stat][:, cols].bitcast(stat_fmt),
+                lhsT_scale=scales[stat][:, cols],
+                rhs=codes[mov][:].bitcast(mov_fmt),
+                rhs_scale=scales[mov][:],
+                start=start,
+                stop=stop,
+            )
+
+        def mm_out1(t, g):
+            bank = psum.tile([P, N_TILE], F32, name="bank")
+            banks[("o1", t, g)] = bank
+            for half in range(2):
+                mx_pass(bank, ("d", half, t), E5M2, g, ("a", half, 0), E4M3, half == 0, half == 1)
+
+        def mm_out0(half, g, first, last):
+            for b in range(4):
+                if first:
+                    banks[("o0", half, b)] = psum.tile([P, N_TILE], F32, name="bank")
+                mx_pass(banks[("o0", half, b)], ("w", g, 0), E4M3, b, ("z", half, g), E5M2, first, last)
+
+        def store(engine, key):
+            result = outs.tile([P, N_TILE], F32, name="result")
+            if engine == "act":
+                nc.scalar.copy(out=result[:], in_=banks[key][:])
+            else:
+                nc.vector.tensor_copy(out=result[:], in_=banks[key][:])
+            view = out0_view if key[0] == "o0" else out1_view
+            nc.sync.dma_start(out=view[key[1], key[2]], in_=result[:])
+
+        def out1_row(t):
+            for g in range(4):
+                mm_out1(t, g)
+                store("act", ("o1", t, g))
+
+        inter_w("act", 0)
+        inter_w("pool", 1)
+        inter_w("pool", 2)
+        inter_w("pool", 3)
+        dz_row(0, 0)
+        turn_dz(0, 0)
+        turned_out(("d", 0, 0))
+        dz_row(0, 1)
+        turn_a(0)
+        turned_out(("a", 0, 0))
+        turn_dz(0, 1)
+        turned_out(("d", 0, 1))
+        dz_row(0, 2)
+        turn_a(1)
+        turned_out(("a", 1, 0))
+        turn_dz(0, 2)
+        turned_out(("d", 0, 2))
+        dz_row(0, 3)
+        turn_dz(0, 3)
+        turned_out(("d", 0, 3))
+        inter_dz("pool", 0, 0)
+        inter_dz("act", 0, 2)
+        dz_row(1, 0)
+        turn_dz(1, 0)
+        turned_out(("d", 1, 0))
+        inter_dz("act", 0, 3)
+        for key in (("a", 0, 0), ("d", 0, 0), ("a", 1, 0), ("d", 1, 0), ("w", 0, 0), ("z", 0, 0), ("w", 2, 0), ("w", 3, 0), ("w", 1, 0)):
+            quant(key)
+        inter_dz("pool", 0, 1, tag="grouped_w10")
+        out1_row(0)
+        mm_out0(0, 0, True, False)
+        dz_row(1, 1)
+        turn_dz(1, 1)
+        turned_out(("d", 1, 1))
+        for key in (("z", 0, 2), ("d", 0, 1), ("z", 0, 3), ("d", 1, 1), ("z", 0, 1)):
+            quant(key)
+        mm_out0(0, 2, False, False)
+        mm_out0(0, 3, False, False)
+        out1_row(1)
+        mm_out0(0, 1, False, True)
+        store("act", ("o0", 0, 0))
+        store("act", ("o0", 0, 1))
+        dz_row(1, 2)
+        turn_dz(1, 2)
+        turned_out(("d", 1, 2))
+        store("act", ("o0", 0, 2))
+        store("act", ("o0", 0, 3))
+        for key in (("d", 0, 2), ("d", 0, 3), ("d", 1, 2)):
+            quant(key)
+        out1_row(2)
+        dz_row(1, 3)
+        turn_dz(1, 3)
+        turned_out(("d", 1, 3))
+        inter_dz("act", 1, 3)
+        inter_dz("dve", 1, 0)
+        quant(("d", 1, 3))
+        out1_row(3)
+        inter_dz("dve", 1, 1)
+        quant(("z", 1, 0))
+        mm_out0(1, 0, True, False)
+        inter_dz("dve", 1, 2)
+        quant(("z", 1, 1))
+        mm_out0(1, 1, False, False)
+        quant(("z", 1, 3))
+        mm_out0(1, 3, False, False)
+        quant(("z", 1, 2))
+        mm_out0(1, 2, False, True)
+        for b in range(4):
+            store("act" if b % 2 == 0 else "dve", ("o0", 1, b))

@@ -32,8 +32,7 @@ def tile_multiscale_gcn_pa_v_kernel(
     with ExitStack() as ctx:
         keep = ctx.enter_context(tc.tile_pool(name="keep", bufs=1))
         outs = ctx.enter_context(tc.tile_pool(name="outs", bufs=8))
-        psum_f = ctx.enter_context(tc.psum_pool(name="psum_f", bufs=1))
-        psum = ctx.enter_context(tc.psum_pool(name="psum", bufs=7))
+        psum = ctx.enter_context(tc.psum_pool(name="psum", bufs=8))
         ctx.enter_context(tc.manual_schedule())
 
         var_sb = keep.tile([P, PACK], BF16, name="var_sb")
@@ -41,39 +40,34 @@ def tile_multiscale_gcn_pa_v_kernel(
         h_sb = keep.tile([P, PACK * V], F32, name="h_sb")
         g_sb = keep.tile([P, PACK * V], BF16, name="g_sb")
         f_sb = keep.tile([P, 4 * PACK * V], BF16, name="f_sb")
-        pa_sb = [keep.tile([P, 4 * N_TILE], BF16, name="pa_sb%d" % i) for i in range(2)]
+        pa_sb = keep.tile([P, 2 * P], BF16, name="pa_sb")
+        pa_sorted = keep.tile([P, P], F32, name="pa_sorted")
+        f_sorted = keep.tile([P, 4 * PACK * V], BF16, name="f_sorted")
         w_sb = [keep.tile([P, PACK * CIN], BF16, name="w_sb%d" % i) for i in range(4)]
         a_sb = [keep.tile([P, 4 * N_TILE], BF16, name="a_sb%d" % i) for i in range(2)]
         dz = [keep.tile([P, PACK * 4 * N_TILE], BF16, name="dz%d" % i) for i in range(2)]
         ident = keep.tile([P, P], F32, name="ident")
 
-        pa_view = PA.rearrange("(g a) (x v) w -> a x g (v w)", a=4, x=2)
         w_view = ada_w.rearrange("(g a) (c t) i -> g (a c) (t i)", a=4, t=PACK)
         a_view = ada_A.rearrange("n (b p) (x v) w -> x p (n b) (v w)", p=P, x=2)
         out0_view = out_0.rearrange("n (b p) (x v) w -> x (n b) p (v w)", p=P, x=2)
         out1_view = out_1.rearrange("(g a) (c t) i -> t g (a c) i", a=4, t=PACK)
 
-        def load_pa(queue, half):
-            for a in range(4):
-                queue.dma_start(
-                    out=pa_sb[half][32 * a : 32 * (a + 1), :].rearrange("p (g c) -> p g c", g=4),
-                    in_=pa_view[a, half].partition_broadcast(32),
-                )
-
+        nc.sync.dma_start(out=pa_sb[:64, :], in_=PA.rearrange("s (b v) w -> (s b) (v w)", b=4))
         nc.sync.dma_start(out=var_sb[:], in_=bn_var.rearrange("(c t) -> c t", t=PACK).partition_broadcast(4))
-        nc.sync.dma_start(
-            out=f_sb[:].rearrange("p (g c) -> p g c", g=4),
-            in_=feat.rearrange("(g a) n (c t) w x -> (a c) g (t w n x)", a=4, t=PACK),
-        )
         nc.sync.dma_start(
             out=h_sb[:], in_=h.rearrange("n (c t) v x -> c (t v n x)", t=PACK).partition_broadcast(4)
         )
-        nc.sync.dma_start(
+        nc.scalar.dma_start(
             out=g_sb[:], in_=grad_out.rearrange("n (c t) v x -> c (t v n x)", t=PACK).partition_broadcast(4)
         )
-        nc.gpsimd.dma_start(out=gamma_sb[:], in_=bn_gamma.rearrange("(c t) -> c t", t=PACK).partition_broadcast(4))
-        load_pa(nc.scalar, 0)
+        nc.scalar.dma_start(out=gamma_sb[:], in_=bn_gamma.rearrange("(c t) -> c t", t=PACK).partition_broadcast(4))
+        nc.scalar.dma_start(
+            out=f_sb[:].rearrange("p (g c) -> p g c", g=4),
+            in_=feat.rearrange("(g a) n (c t) w x -> (a c) g (t w n x)", a=4, t=PACK),
+        )
         make_identity(nc, ident[:])
+        nc.vector.memset(pa_sorted[64:, :], 0.0)
 
         def load_w(g):
             nc.sync.dma_start(out=w_sb[g][:], in_=w_view[g])
@@ -87,7 +81,6 @@ def tile_multiscale_gcn_pa_v_kernel(
         load_w(2)
         load_a(1)
         load_w(3)
-        load_pa(nc.sync, 1)
 
         std = keep.tile([P, PACK], F32, name="std")
         rstd = keep.tile([P, PACK], F32, name="rstd")
@@ -96,17 +89,30 @@ def tile_multiscale_gcn_pa_v_kernel(
         dy = keep.tile([P, PACK * V], F32, name="dy")
         nc.scalar.activation(out=std[:], in_=var_sb[:], func=ACT.Sqrt, bias=EPS)
 
-        f_turned_ps = psum.tile([P, N_TILE], F32, name="bank")
-        f_turned = keep.tile([P, 2 * P], F32, name="f_turned")
-        f_ps = psum_f.tile([P, N_TILE], F32, name="f_ps")
-        for b in range(2):
-            cols = slice(b * P, (b + 1) * P)
-            nc.tensor.transpose(f_turned_ps[:, cols], f_sb[:].bitcast(F32)[:, cols], ident[:])
-        nc.scalar.copy(out=f_turned[:], in_=f_turned_ps[:, : 2 * P])
-        for b in range(2):
-            cols = slice(b * P, (b + 1) * P)
-            nc.tensor.transpose(f_ps[:, cols], f_turned[:, cols], ident[:])
-        f_gtw = f_ps[:, : 2 * P].bitcast(BF16).rearrange("p (g t w) -> p g t w", g=4, t=PACK)
+        nc.vector.tensor_copy(
+            out=pa_sorted[:64, :].rearrange("p (v u c) -> p v u c", v=8, u=2),
+            in_=pa_sb[:64, :].bitcast(F32).rearrange("p (v c u) -> p v u c", v=8, u=2),
+        )
+        pa_turned = psum.tile([P, N_TILE], F32, name="bank")
+        nc.tensor.transpose(pa_turned[:, :P], pa_sorted[:], ident[:])
+        pa_wide = []
+        for b in range(4):
+            wide = keep.tile([P, N_TILE], F32, name="pa_wide%d" % b)
+            pa_wide.append(wide)
+            nc.scalar.copy(
+                out=wide[:].rearrange("p (s c) -> p s c", s=S),
+                in_=pa_turned[:, b:64:4].unsqueeze(2).to_broadcast([P, S, 32]),
+            )
+        pa_banks = {}
+
+        def spread_pa(b):
+            pa_banks[b] = psum.tile([P, N_TILE], F32, name="bank")
+            for g in range(4):
+                cols = slice(g * P, (g + 1) * P)
+                nc.tensor.transpose(pa_banks[b][:, cols], pa_wide[b][:, cols], ident[:])
+
+        spread_pa(0)
+        spread_pa(1)
 
         def by_tv(ap):
             return ap.rearrange("p (t v) -> p t v", t=PACK)
@@ -116,6 +122,10 @@ def tile_multiscale_gcn_pa_v_kernel(
 
         nc.vector.scalar_tensor_tensor(
             out=masked[:], in0=h_sb[:], scalar=0.0, in1=g_sb[:], op0=ALU.is_gt, op1=ALU.mult
+        )
+        nc.vector.tensor_copy(
+            out=f_sorted[:].bitcast(F32).rearrange("p (t g u c) -> p t g u c", t=PACK, g=4, u=2),
+            in_=f_sb[:].bitcast(F32).rearrange("p (g t c u) -> p t g u c", t=PACK, g=4, u=2),
         )
         nc.vector.reciprocal(out=rstd[:], in_=std[:])
         nc.vector.tensor_tensor(out=by_tv(gained[:]), in0=by_tv(masked[:]), in1=over_v(gamma_sb[:]), op=ALU.mult)
@@ -133,22 +143,23 @@ def tile_multiscale_gcn_pa_v_kernel(
             return grouped[key]
 
         def dz_row(half, t):
-            dz_view = dz[half][:].rearrange("p (t g v w) -> p t g v w", t=PACK, g=4, v=HALF_V)
-            pa_gvw = pa_sb[half][:].rearrange("p (g v w) -> p g v w", g=4, v=HALF_V)
+            dz_view = dz[half][:].rearrange("p (t g u v c) -> p t v g u c", t=PACK, g=4, u=2, v=HALF_V)
+            f_row = f_sorted[:, t * P : (t + 1) * P].rearrange("p (g u c) -> p g u c", g=4, u=2)
             for v in range(HALF_V):
                 col = t * V + half * HALF_V + v
+                pa_bank = pa_banks[2 * half + v // 8][:].bitcast(BF16)
                 nc.vector.scalar_tensor_tensor(
-                    out=dz_view[:, t, :, v, :],
-                    in0=f_gtw[:, :, t, :],
+                    out=dz_view[:, t, v],
+                    in0=f_row,
                     scalar=dy[:, col : col + 1],
-                    in1=pa_gvw[:, :, v, :],
+                    in1=pa_bank.rearrange("p (g v u c) -> p v g u c", g=4, v=8, u=2)[:, v % 8],
                     op0=ALU.mult,
                     op1=ALU.mult,
                 )
 
         banks = {}
 
-        def turn(key, words):
+        def turn(key, words, paired):
             for j in range(2):
                 bank = psum.tile([P, N_TILE], F32, name="bank")
                 banks[key + (j,)] = bank
@@ -156,15 +167,17 @@ def tile_multiscale_gcn_pa_v_kernel(
                     for u in range(2):
                         base = (2 * j + a) * 2 * P
                         slot = (2 * a + u) * P
-                        nc.tensor.transpose(
-                            bank[:, slot : slot + P], words[:, base + u : base + 2 * P : 2], ident[:]
-                        )
+                        if paired:
+                            src = words[:, base + u : base + 2 * P : 2]
+                        else:
+                            src = words[:, base + u * P : base + (u + 1) * P]
+                        nc.tensor.transpose(bank[:, slot : slot + P], src, ident[:])
 
         def turn_dz(half, t):
-            turn(("d", half, t), dz[half][:].bitcast(F32)[:, t * 2 * N_TILE : (t + 1) * 2 * N_TILE])
+            turn(("d", half, t), dz[half][:].bitcast(F32)[:, t * 2 * N_TILE : (t + 1) * 2 * N_TILE], False)
 
         def turn_a(half):
-            turn(("a", half, 0), a_sb[half][:].bitcast(F32))
+            turn(("a", half, 0), a_sb[half][:].bitcast(F32), True)
 
         def turned_out(key):
             dst = new_grouped(key)[:].bitcast(F32).rearrange("p (j a r u) -> p j a r u", j=2, a=2, u=2)
@@ -232,10 +245,14 @@ def tile_multiscale_gcn_pa_v_kernel(
 
         def store(engine, key):
             result = outs.tile([P, N_TILE], F32, name="result")
+            src, dst = banks[key][:], result[:]
+            if key[0] == "o0":
+                src = src.rearrange("p (u m e) -> p m u e", u=2, e=2)
+                dst = dst.rearrange("p (m u e) -> p m u e", u=2, e=2)
             if engine == "act":
-                nc.scalar.copy(out=result[:], in_=banks[key][:])
+                nc.scalar.copy(out=dst, in_=src)
             else:
-                nc.vector.tensor_copy(out=result[:], in_=banks[key][:])
+                nc.vector.tensor_copy(out=dst, in_=src)
             view = out0_view if key[0] == "o0" else out1_view
             nc.sync.dma_start(out=view[key[1], key[2]], in_=result[:])
 
@@ -245,71 +262,86 @@ def tile_multiscale_gcn_pa_v_kernel(
                 store("act", ("o1", t, g))
 
         inter_w("act", 0)
-        inter_w("pool", 1)
-        inter_w("pool", 2)
-        inter_w("pool", 3)
         dz_row(0, 0)
         turn_dz(0, 0)
         turned_out(("d", 0, 0))
+        inter_w("act", 1)
         dz_row(0, 1)
         turn_a(0)
         turned_out(("a", 0, 0))
         turn_dz(0, 1)
         turned_out(("d", 0, 1))
-        dz_row(0, 2)
         turn_a(1)
         turned_out(("a", 1, 0))
+        dz_row(0, 2)
+        inter_w("act", 2)
         turn_dz(0, 2)
         turned_out(("d", 0, 2))
+        spread_pa(2)
+        spread_pa(3)
         dz_row(0, 3)
         turn_dz(0, 3)
+        inter_dz("act", 0, 1)
         turned_out(("d", 0, 3))
-        inter_dz("pool", 0, 0)
-        inter_dz("act", 0, 2)
         dz_row(1, 0)
         turn_dz(1, 0)
         turned_out(("d", 1, 0))
-        inter_dz("act", 0, 3)
-        for key in (("a", 0, 0), ("d", 0, 0), ("a", 1, 0), ("d", 1, 0), ("w", 0, 0), ("z", 0, 0), ("w", 2, 0), ("w", 3, 0), ("w", 1, 0)):
-            quant(key)
-        inter_dz("pool", 0, 1, tag="grouped_w10")
+        quant(("a", 0, 0))
+        quant(("a", 1, 0))
+        quant(("d", 0, 0))
+        inter_dz("dve", 0, 0)
+        quant(("w", 0, 0))
+        quant(("d", 1, 0))
+        inter_dz("act", 0, 2)
         out1_row(0)
-        mm_out0(0, 0, True, False)
+        quant(("w", 1, 0))
+        quant(("z", 0, 0))
+        quant(("z", 0, 1))
+        mm_out0(0, 1, True, False)
+        mm_out0(0, 0, False, False)
+        inter_w("act", 3)
         dz_row(1, 1)
         turn_dz(1, 1)
         turned_out(("d", 1, 1))
-        for key in (("z", 0, 2), ("d", 0, 1), ("z", 0, 3), ("d", 1, 1), ("z", 0, 1)):
-            quant(key)
+        inter_dz("act", 0, 3)
+        quant(("w", 2, 0))
+        quant(("z", 0, 2))
+        quant(("d", 0, 1))
         mm_out0(0, 2, False, False)
-        mm_out0(0, 3, False, False)
+        quant(("d", 1, 1))
         out1_row(1)
-        mm_out0(0, 1, False, True)
-        store("act", ("o0", 0, 0))
-        store("act", ("o0", 0, 1))
         dz_row(1, 2)
         turn_dz(1, 2)
         turned_out(("d", 1, 2))
+        quant(("w", 3, 0))
+        quant(("z", 0, 3))
+        mm_out0(0, 3, False, True)
+        store("act", ("o0", 0, 0))
+        store("act", ("o0", 0, 1))
         store("act", ("o0", 0, 2))
         store("act", ("o0", 0, 3))
-        for key in (("d", 0, 2), ("d", 0, 3), ("d", 1, 2)):
-            quant(key)
+        quant(("d", 0, 2))
+        quant(("d", 1, 2))
         out1_row(2)
         dz_row(1, 3)
         turn_dz(1, 3)
         turned_out(("d", 1, 3))
         inter_dz("act", 1, 3)
+        quant(("d", 0, 3))
         inter_dz("dve", 1, 0)
         quant(("d", 1, 3))
-        out1_row(3)
-        inter_dz("dve", 1, 1)
         quant(("z", 1, 0))
+        out1_row(3)
         mm_out0(1, 0, True, False)
-        inter_dz("dve", 1, 2)
+        inter_dz("dve", 1, 1)
         quant(("z", 1, 1))
         mm_out0(1, 1, False, False)
+        inter_dz("dve", 1, 2)
         quant(("z", 1, 3))
         mm_out0(1, 3, False, False)
         quant(("z", 1, 2))
         mm_out0(1, 2, False, True)
-        for b in range(4):
-            store("act" if b % 2 == 0 else "dve", ("o0", 1, b))
+        store("act", ("o0", 1, 0))
+        store("dve", ("o0", 1, 1))
+        store("act", ("o0", 1, 2))
+        store("dve", ("o0", 1, 3))

@@ -265,54 +265,62 @@ def tile_multiscale_gcn_pa_v_kernel(
         dz_row(0, 0)
         turn_dz(0, 0)
         turned_out(("d", 0, 0))
+        inter_w("pool", 2)
+        inter_w("pool", 3)
         inter_w("act", 1)
         dz_row(0, 1)
         turn_a(0)
         turned_out(("a", 0, 0))
         turn_dz(0, 1)
         turned_out(("d", 0, 1))
-        turn_a(1)
-        turned_out(("a", 1, 0))
-        dz_row(0, 2)
-        inter_w("act", 2)
-        turn_dz(0, 2)
-        turned_out(("d", 0, 2))
         spread_pa(2)
         spread_pa(3)
+        dz_row(0, 2)
+        turn_a(1)
+        turned_out(("a", 1, 0))
+        turn_dz(0, 2)
+        turned_out(("d", 0, 2))
         dz_row(0, 3)
+        inter_dz("pool", 0, 3)
+        inter_dz("act", 0, 0)
         turn_dz(0, 3)
-        inter_dz("act", 0, 1)
         turned_out(("d", 0, 3))
         dz_row(1, 0)
         turn_dz(1, 0)
         turned_out(("d", 1, 0))
-        quant(("a", 0, 0))
-        quant(("a", 1, 0))
-        quant(("d", 0, 0))
-        inter_dz("dve", 0, 0)
-        quant(("w", 0, 0))
-        quant(("d", 1, 0))
-        inter_dz("act", 0, 2)
-        out1_row(0)
-        quant(("w", 1, 0))
-        quant(("z", 0, 0))
-        quant(("z", 0, 1))
-        mm_out0(0, 1, True, False)
-        mm_out0(0, 0, False, False)
-        inter_w("act", 3)
+        inter_dz("act", 0, 1)
         dz_row(1, 1)
         turn_dz(1, 1)
         turned_out(("d", 1, 1))
-        inter_dz("act", 0, 3)
-        quant(("w", 2, 0))
-        quant(("z", 0, 2))
-        quant(("d", 0, 1))
-        mm_out0(0, 2, False, False)
-        quant(("d", 1, 1))
-        out1_row(1)
+        inter_dz("act", 0, 2)
         dz_row(1, 2)
         turn_dz(1, 2)
         turned_out(("d", 1, 2))
+        quant(("d", 0, 0))
+        quant(("a", 0, 0))
+        quant(("d", 1, 0))
+        quant(("a", 1, 0))
+        out1_row(0)
+        quant(("d", 0, 1))
+        quant(("d", 1, 1))
+        out1_row(1)
+        dz_row(1, 3)
+        turn_dz(1, 3)
+        turned_out(("d", 1, 3))
+        quant(("d", 0, 2))
+        quant(("d", 1, 2))
+        out1_row(2)
+        inter_dz("act", 1, 3)
+        quant(("w", 0, 0))
+        quant(("z", 0, 0))
+        mm_out0(0, 0, True, False)
+        quant(("w", 1, 0))
+        quant(("z", 0, 1))
+        mm_out0(0, 1, False, False)
+        inter_dz("dve", 1, 0)
+        quant(("w", 2, 0))
+        quant(("z", 0, 2))
+        mm_out0(0, 2, False, False)
         quant(("w", 3, 0))
         quant(("z", 0, 3))
         mm_out0(0, 3, False, True)
@@ -320,25 +328,17 @@ def tile_multiscale_gcn_pa_v_kernel(
         store("act", ("o0", 0, 1))
         store("act", ("o0", 0, 2))
         store("act", ("o0", 0, 3))
-        quant(("d", 0, 2))
-        quant(("d", 1, 2))
-        out1_row(2)
-        dz_row(1, 3)
-        turn_dz(1, 3)
-        turned_out(("d", 1, 3))
-        inter_dz("act", 1, 3)
         quant(("d", 0, 3))
-        inter_dz("dve", 1, 0)
         quant(("d", 1, 3))
-        quant(("z", 1, 0))
         out1_row(3)
-        mm_out0(1, 0, True, False)
         inter_dz("dve", 1, 1)
-        quant(("z", 1, 1))
-        mm_out0(1, 1, False, False)
-        inter_dz("dve", 1, 2)
+        quant(("z", 1, 0))
+        mm_out0(1, 0, True, False)
         quant(("z", 1, 3))
         mm_out0(1, 3, False, False)
+        inter_dz("dve", 1, 2)
+        quant(("z", 1, 1))
+        mm_out0(1, 1, False, False)
         quant(("z", 1, 2))
         mm_out0(1, 2, False, True)
         store("act", ("o0", 1, 0))

@@ -14,10 +14,20 @@ ACT = mybir.ActivationFunctionType
 
 CIN, COUT, V, S = 512, 128, 32, 16
 EPS = 1e-5
+
 P = 128
-PACK = 4
-N_TILE = 512
-HALF_V = 16
+PLACES = 4
+BANK = 512
+PASSES = S * COUT // (P * PLACES)
+HALVES = V * V // (P * PLACES)
+S_PASS = S // PASSES
+O_PARTS = P // S_PASS
+HALF_V = V // HALVES
+BANK_V = 8
+PA_BANKS = V // BANK_V
+PA_ROWS = S * PA_BANKS
+I_TILES = CIN // P
+RESULT_BUFS = 8
 
 FLOPS = 2 * 2 * (S * COUT) * CIN * (V * V)
 BYTES = 2 * (CIN * V * V + S * COUT * CIN + S * V * V + S * COUT * V + 2 * COUT + COUT * V) + 4 * (
@@ -31,49 +41,51 @@ def tile_multiscale_gcn_pa_v_kernel(
     nc = tc.nc
     with ExitStack() as ctx:
         keep = ctx.enter_context(tc.tile_pool(name="keep", bufs=1))
-        outs = ctx.enter_context(tc.tile_pool(name="outs", bufs=8))
+        outs = ctx.enter_context(tc.tile_pool(name="outs", bufs=RESULT_BUFS))
         psum = ctx.enter_context(tc.psum_pool(name="psum", bufs=8))
         ctx.enter_context(tc.manual_schedule())
 
-        var_sb = keep.tile([P, PACK], BF16, name="var_sb")
-        gamma_sb = keep.tile([P, PACK], BF16, name="gamma_sb")
-        h_sb = keep.tile([P, PACK * V], F32, name="h_sb")
-        g_sb = keep.tile([P, PACK * V], BF16, name="g_sb")
-        f_sb = keep.tile([P, 4 * PACK * V], BF16, name="f_sb")
-        pa_sb = keep.tile([P, 2 * P], BF16, name="pa_sb")
+        var_sb = keep.tile([P, PLACES], BF16, name="var_sb")
+        gamma_sb = keep.tile([P, PLACES], BF16, name="gamma_sb")
+        h_sb = keep.tile([P, PLACES * V], F32, name="h_sb")
+        grad_sb = keep.tile([P, PLACES * V], BF16, name="grad_sb")
+        f_sb = keep.tile([P, PASSES * PLACES * V], BF16, name="f_sb")
+        pa_sb = keep.tile([P, BANK_V * V], BF16, name="pa_sb")
         pa_sorted = keep.tile([P, P], F32, name="pa_sorted")
-        f_sorted = keep.tile([P, 4 * PACK * V], BF16, name="f_sorted")
-        w_sb = [keep.tile([P, PACK * CIN], BF16, name="w_sb%d" % i) for i in range(4)]
-        a_sb = [keep.tile([P, 4 * N_TILE], BF16, name="a_sb%d" % i) for i in range(2)]
-        dz = [keep.tile([P, PACK * 4 * N_TILE], BF16, name="dz%d" % i) for i in range(2)]
+        f_sorted = keep.tile([P, PASSES * PLACES * V], BF16, name="f_sorted")
+        w_sb = [keep.tile([P, PLACES * CIN], BF16, name="w_sb%d" % g) for g in range(PASSES)]
+        a_sb = [keep.tile([P, I_TILES * BANK], BF16, name="a_sb%d" % half) for half in range(HALVES)]
+        dz = [keep.tile([P, PLACES * PASSES * BANK], BF16, name="dz%d" % half) for half in range(HALVES)]
         ident = keep.tile([P, P], F32, name="ident")
 
-        w_view = ada_w.rearrange("(g a) (c t) i -> g (a c) (t i)", a=4, t=PACK)
-        a_view = ada_A.rearrange("n (b p) (x v) w -> x p (n b) (v w)", p=P, x=2)
-        out0_view = out_0.rearrange("n (b p) (x v) w -> x (n b) p (v w)", p=P, x=2)
-        out1_view = out_1.rearrange("(g a) (c t) i -> t g (a c) i", a=4, t=PACK)
+        w_view = ada_w.rearrange("(g a) (c t) i -> g (a c) (t i)", a=S_PASS, t=PLACES)
+        a_view = ada_A.rearrange("n (b p) (x v) w -> x p (n b) (v w)", p=P, x=HALVES)
+        out0_view = out_0.rearrange("n (b p) (x v) w -> x (n b) p (v w)", p=P, x=HALVES)
+        out1_view = out_1.rearrange("(g a) (c t) i -> t g (a c) i", a=S_PASS, t=PLACES)
 
-        nc.sync.dma_start(out=pa_sb[:64, :], in_=PA.rearrange("s (b v) w -> (s b) (v w)", b=4))
-        nc.sync.dma_start(out=var_sb[:], in_=bn_var.rearrange("(c t) -> c t", t=PACK).partition_broadcast(4))
-        nc.sync.dma_start(
-            out=h_sb[:], in_=h.rearrange("n (c t) v x -> c (t v n x)", t=PACK).partition_broadcast(4)
-        )
+        def per_channel(vec):
+            return vec.rearrange("(c t) -> c t", t=PLACES).partition_broadcast(S_PASS)
+
+        def per_channel_and_joint(x):
+            return x.rearrange("n (c t) v x -> c (t v n x)", t=PLACES).partition_broadcast(S_PASS)
+
+        nc.sync.dma_start(out=pa_sb[:PA_ROWS, :], in_=PA.rearrange("s (b v) w -> (s b) (v w)", b=PA_BANKS))
+        nc.sync.dma_start(out=var_sb[:], in_=per_channel(bn_var))
+        nc.sync.dma_start(out=h_sb[:], in_=per_channel_and_joint(h))
         nc.scalar.dma_start(
-            out=g_sb[:], in_=grad_out.rearrange("n (c t) v x -> c (t v n x)", t=PACK).partition_broadcast(4)
+            out=f_sb[:].rearrange("p (g c) -> p g c", g=PASSES),
+            in_=feat.rearrange("(g a) n (c t) w x -> (a c) g (t w n x)", a=S_PASS, t=PLACES),
         )
-        nc.scalar.dma_start(out=gamma_sb[:], in_=bn_gamma.rearrange("(c t) -> c t", t=PACK).partition_broadcast(4))
-        nc.scalar.dma_start(
-            out=f_sb[:].rearrange("p (g c) -> p g c", g=4),
-            in_=feat.rearrange("(g a) n (c t) w x -> (a c) g (t w n x)", a=4, t=PACK),
-        )
+        nc.scalar.dma_start(out=grad_sb[:], in_=per_channel_and_joint(grad_out))
+        nc.scalar.dma_start(out=gamma_sb[:], in_=per_channel(bn_gamma))
         make_identity(nc, ident[:])
-        nc.vector.memset(pa_sorted[64:, :], 0.0)
+        nc.vector.memset(pa_sorted[PA_ROWS:, :], 0.0)
 
         def load_w(g):
             nc.sync.dma_start(out=w_sb[g][:], in_=w_view[g])
 
         def load_a(half):
-            nc.sync.dma_start(out=a_sb[half][:].rearrange("p (b c) -> p b c", b=4), in_=a_view[half])
+            nc.sync.dma_start(out=a_sb[half][:].rearrange("p (b c) -> p b c", b=I_TILES), in_=a_view[half])
 
         load_w(0)
         load_w(1)
@@ -82,116 +94,112 @@ def tile_multiscale_gcn_pa_v_kernel(
         load_a(1)
         load_w(3)
 
-        std = keep.tile([P, PACK], F32, name="std")
-        rstd = keep.tile([P, PACK], F32, name="rstd")
-        masked = keep.tile([P, PACK * V], F32, name="masked")
-        gained = keep.tile([P, PACK * V], F32, name="gained")
-        dy = keep.tile([P, PACK * V], F32, name="dy")
+        std = keep.tile([P, PLACES], F32, name="std")
+        rstd = keep.tile([P, PLACES], F32, name="rstd")
+        masked = keep.tile([P, PLACES * V], F32, name="masked")
+        gained = keep.tile([P, PLACES * V], F32, name="gained")
+        dy = keep.tile([P, PLACES * V], F32, name="dy")
         nc.scalar.activation(out=std[:], in_=var_sb[:], func=ACT.Sqrt, bias=EPS)
 
         nc.vector.tensor_copy(
-            out=pa_sorted[:64, :].rearrange("p (v u c) -> p v u c", v=8, u=2),
-            in_=pa_sb[:64, :].bitcast(F32).rearrange("p (v c u) -> p v u c", v=8, u=2),
+            out=pa_sorted[:PA_ROWS, :].rearrange("p (v u c) -> p v u c", v=BANK_V, u=2),
+            in_=pa_sb[:PA_ROWS, :].bitcast(F32).rearrange("p (v c u) -> p v u c", v=BANK_V, u=2),
         )
-        pa_turned = psum.tile([P, N_TILE], F32, name="bank")
+        pa_turned = psum.tile([P, BANK], F32, name="bank")
         nc.tensor.transpose(pa_turned[:, :P], pa_sorted[:], ident[:])
         pa_wide = []
-        for b in range(4):
-            wide = keep.tile([P, N_TILE], F32, name="pa_wide%d" % b)
+        for b in range(PA_BANKS):
+            wide = keep.tile([P, BANK], F32, name="pa_wide%d" % b)
             pa_wide.append(wide)
-            nc.scalar.copy(
-                out=wide[:].rearrange("p (s c) -> p s c", s=S),
-                in_=pa_turned[:, b:64:4].unsqueeze(2).to_broadcast([P, S, 32]),
-            )
-        pa_banks = {}
-
-        def spread_pa(b):
-            pa_banks[b] = psum.tile([P, N_TILE], F32, name="bank")
-            for g in range(4):
+            s_part = S // 2 if b == 0 else S
+            for s0 in range(0, S, s_part):
+                columns = pa_turned[:, PA_BANKS * s0 + b : PA_BANKS * (s0 + s_part) : PA_BANKS]
+                nc.scalar.copy(
+                    out=wide[:].rearrange("p (s c) -> p s c", s=S)[:, s0 : s0 + s_part],
+                    in_=columns.unsqueeze(2).to_broadcast([P, s_part, O_PARTS]),
+                )
+        pa_banks = []
+        for b in range(PA_BANKS):
+            pa_banks.append(psum.tile([P, BANK], F32, name="bank"))
+            for g in range(PASSES):
                 cols = slice(g * P, (g + 1) * P)
                 nc.tensor.transpose(pa_banks[b][:, cols], pa_wide[b][:, cols], ident[:])
 
-        spread_pa(0)
-        spread_pa(1)
+        def by_place(ap):
+            return ap.rearrange("p (t v) -> p t v", t=PLACES)
 
-        def by_tv(ap):
-            return ap.rearrange("p (t v) -> p t v", t=PACK)
-
-        def over_v(ap):
-            return ap.unsqueeze(2).to_broadcast([P, PACK, V])
+        def over_joints(ap):
+            return ap.unsqueeze(2).to_broadcast([P, PLACES, V])
 
         nc.vector.scalar_tensor_tensor(
-            out=masked[:], in0=h_sb[:], scalar=0.0, in1=g_sb[:], op0=ALU.is_gt, op1=ALU.mult
+            out=masked[:], in0=h_sb[:], scalar=0.0, in1=grad_sb[:], op0=ALU.is_gt, op1=ALU.mult
         )
         nc.vector.tensor_copy(
-            out=f_sorted[:].bitcast(F32).rearrange("p (t g u c) -> p t g u c", t=PACK, g=4, u=2),
-            in_=f_sb[:].bitcast(F32).rearrange("p (g t c u) -> p t g u c", t=PACK, g=4, u=2),
+            out=f_sorted[:].bitcast(F32).rearrange("p (t g u c) -> p t g u c", t=PLACES, g=PASSES, u=2),
+            in_=f_sb[:].bitcast(F32).rearrange("p (g t c u) -> p t g u c", t=PLACES, g=PASSES, u=2),
+        )
+        nc.vector.tensor_tensor(
+            out=by_place(gained[:]), in0=by_place(masked[:]), in1=over_joints(gamma_sb[:]), op=ALU.mult
         )
         nc.vector.reciprocal(out=rstd[:], in_=std[:])
-        nc.vector.tensor_tensor(out=by_tv(gained[:]), in0=by_tv(masked[:]), in1=over_v(gamma_sb[:]), op=ALU.mult)
-        nc.vector.tensor_tensor(out=by_tv(dy[:]), in0=by_tv(gained[:]), in1=over_v(rstd[:]), op=ALU.mult)
+        nc.vector.tensor_tensor(out=by_place(dy[:]), in0=by_place(gained[:]), in1=over_joints(rstd[:]), op=ALU.mult)
+
+        def dz_row(half, t):
+            dz_view = dz[half][:].rearrange("p (t g u v c) -> p t v g u c", t=PLACES, g=PASSES, u=2, v=HALF_V)
+            f_row = f_sorted[:, t * P : (t + 1) * P].rearrange("p (g u c) -> p g u c", g=PASSES, u=2)
+            for v in range(HALF_V):
+                joint = half * HALF_V + v
+                pa_bank = pa_banks[joint // BANK_V][:].bitcast(BF16)
+                pa_view = pa_bank.rearrange("p (g v u c) -> p v g u c", g=PASSES, v=BANK_V, u=2)
+                nc.vector.scalar_tensor_tensor(
+                    out=dz_view[:, t, v],
+                    in0=f_row,
+                    scalar=dy[:, t * V + joint : t * V + joint + 1],
+                    in1=pa_view[:, joint % BANK_V],
+                    op0=ALU.mult,
+                    op1=ALU.mult,
+                )
 
         grouped = {}
         codes = {}
         scales = {}
 
-        def new_grouped(key, tag=None):
-            grouped[key] = keep.tile(
-                [P, PACK * N_TILE], BF16, name="grouped_%s%d%d" % key, tag=tag or ("grouped_%s%d%d" % key),
-                align_bytes=64,
-            )
+        def label(key):
+            return "_".join(str(part) for part in key)
+
+        def new_grouped(key):
+            grouped[key] = keep.tile([P, BANK * PLACES], BF16, name="grouped_" + label(key), align_bytes=64)
             return grouped[key]
 
-        def dz_row(half, t):
-            dz_view = dz[half][:].rearrange("p (t g u v c) -> p t v g u c", t=PACK, g=4, u=2, v=HALF_V)
-            f_row = f_sorted[:, t * P : (t + 1) * P].rearrange("p (g u c) -> p g u c", g=4, u=2)
-            for v in range(HALF_V):
-                col = t * V + half * HALF_V + v
-                pa_bank = pa_banks[2 * half + v // 8][:].bitcast(BF16)
-                nc.vector.scalar_tensor_tensor(
-                    out=dz_view[:, t, v],
-                    in0=f_row,
-                    scalar=dy[:, col : col + 1],
-                    in1=pa_bank.rearrange("p (g v u c) -> p v g u c", g=4, v=8, u=2)[:, v % 8],
-                    op0=ALU.mult,
-                    op1=ALU.mult,
-                )
-
-        banks = {}
-
-        def turn(key, words, paired):
-            for j in range(2):
-                bank = psum.tile([P, N_TILE], F32, name="bank")
-                banks[key + (j,)] = bank
-                for a in range(2):
+        def turn(key, block_words):
+            turned = []
+            for pair in range(2):
+                bank = psum.tile([P, BANK], F32, name="bank")
+                turned.append(bank)
+                for j in range(2):
                     for u in range(2):
-                        base = (2 * j + a) * 2 * P
-                        slot = (2 * a + u) * P
-                        if paired:
-                            src = words[:, base + u : base + 2 * P : 2]
-                        else:
-                            src = words[:, base + u * P : base + (u + 1) * P]
-                        nc.tensor.transpose(bank[:, slot : slot + P], src, ident[:])
+                        slot = (2 * j + u) * P
+                        nc.tensor.transpose(bank[:, slot : slot + P], block_words(2 * pair + j, u), ident[:])
+            dst = new_grouped(key)[:].bitcast(F32).rearrange("p (x j r u) -> p x j r u", x=2, j=2, u=2)
+            for pair in range(2):
+                src = turned[pair][:].rearrange("p (j u r) -> p j r u", j=2, u=2)
+                nc.scalar.copy(out=dst[:, pair], in_=src)
 
         def turn_dz(half, t):
-            turn(("d", half, t), dz[half][:].bitcast(F32)[:, t * 2 * N_TILE : (t + 1) * 2 * N_TILE], False)
+            words = dz[half][:].bitcast(F32)
+            turn(("dz1", half, t), lambda g, u: words[:, ((t * PASSES + g) * 2 + u) * P :][:, :P])
 
         def turn_a(half):
-            turn(("a", half, 0), a_sb[half][:].bitcast(F32), True)
+            words = a_sb[half][:].bitcast(F32)
+            turn(("a", half), lambda b, u: words[:, 2 * P * b + u : 2 * P * (b + 1) : 2])
 
-        def turned_out(key):
-            dst = new_grouped(key)[:].bitcast(F32).rearrange("p (j a r u) -> p j a r u", j=2, a=2, u=2)
-            for j in range(2):
-                src = banks[key + (j,)][:].rearrange("p (a u r) -> p a r u", a=2, u=2)
-                nc.scalar.copy(out=dst[:, j], in_=src)
-
-        def interleave(engine, key, rows, tag=None):
-            tile = new_grouped(key, tag)
-            if engine == "pool":
-                for j in range(2):
-                    cols = slice(j * N_TILE // 2, (j + 1) * N_TILE // 2)
+        def interleave(engine, key, rows):
+            tile = new_grouped(key)
+            if engine == "gpsimd":
+                for c0 in range(0, BANK, BANK // 2):
+                    cols = slice(c0, c0 + BANK // 2)
                     nc.gpsimd.tensor_scalar(
-                        out=tile[:].rearrange("p (c t) -> p c t", t=PACK)[:, cols, :],
+                        out=tile[:].rearrange("p (c t) -> p c t", t=PLACES)[:, cols, :],
                         in0=rows.rearrange("p t c -> p c t")[:, cols, :],
                         scalar1=1.0,
                         scalar2=0.0,
@@ -199,149 +207,130 @@ def tile_multiscale_gcn_pa_v_kernel(
                         op1=ALU.add,
                     )
                 return
-            dst = tile[:].rearrange("p (c i t) -> p c t i", i=4, t=PACK)
+            dst = tile[:].rearrange("p (c i t) -> p c t i", i=4, t=PLACES)
             src = rows.rearrange("p t (c i) -> p c t i", i=4)
-            if engine == "act":
+            if engine == "scalar":
                 nc.scalar.copy(out=dst, in_=src)
             else:
                 nc.vector.tensor_copy(out=dst, in_=src)
 
-        def inter_w(engine, g):
-            interleave(engine, ("w", g, 0), w_sb[g][:].rearrange("p (t c) -> p t c", t=PACK))
+        def interleave_w(engine, g):
+            interleave(engine, ("w", g), w_sb[g][:].rearrange("p (t c) -> p t c", t=PLACES))
 
-        def inter_dz(engine, half, g, tag=None):
-            rows = dz[half][:].rearrange("p (t g c) -> p g t c", t=PACK, g=4)[:, g]
-            interleave(engine, ("z", half, g), rows, tag)
+        def interleave_dz(engine, half, g):
+            rows = dz[half][:].rearrange("p (t g c) -> p g t c", t=PLACES, g=PASSES)[:, g]
+            interleave(engine, ("dz0", half, g), rows)
 
-        def quant(key):
-            fmt = E4M3 if key[0] in "wa" else E5M2
-            codes[key] = keep.tile([P, N_TILE], U32, name="codes_%s%d%d" % key, align_bytes=64)
-            scales[key] = keep.tile([P, N_TILE], U8, name="scales_%s%d%d" % key, align_bytes=64)
-            nc.vector.quantize_mx(out=codes[key][:].bitcast(fmt), scales=scales[key][:], in_=grouped[key][:])
+        def fmt(key):
+            return E4M3 if key[0] in ("w", "a") else E5M2
 
-        def mx_pass(bank, stat, stat_fmt, block, mov, mov_fmt, start, stop):
-            cols = slice(block * P, (block + 1) * P)
+        def quantize(key):
+            codes[key] = keep.tile([P, BANK], U32, name="codes_" + label(key), align_bytes=64)
+            scales[key] = keep.tile([P, BANK], U8, name="scales_" + label(key), align_bytes=64)
+            nc.vector.quantize_mx(out=codes[key][:].bitcast(fmt(key)), scales=scales[key][:], in_=grouped[key][:])
+
+        def mx_pass(bank, stationary, j, moving, start, stop):
+            cols = slice(j * P, (j + 1) * P)
             nc.tensor.matmul_mx(
                 out=bank[:],
-                lhsT=codes[stat][:, cols].bitcast(stat_fmt),
-                lhsT_scale=scales[stat][:, cols],
-                rhs=codes[mov][:].bitcast(mov_fmt),
-                rhs_scale=scales[mov][:],
+                lhsT=codes[stationary][:, cols].bitcast(fmt(stationary)),
+                lhsT_scale=scales[stationary][:, cols],
+                rhs=codes[moving][:].bitcast(fmt(moving)),
+                rhs_scale=scales[moving][:],
                 start=start,
                 stop=stop,
             )
 
-        def mm_out1(t, g):
-            bank = psum.tile([P, N_TILE], F32, name="bank")
-            banks[("o1", t, g)] = bank
-            for half in range(2):
-                mx_pass(bank, ("d", half, t), E5M2, g, ("a", half, 0), E4M3, half == 0, half == 1)
-
-        def mm_out0(half, g, first, last):
-            for b in range(4):
-                if first:
-                    banks[("o0", half, b)] = psum.tile([P, N_TILE], F32, name="bank")
-                mx_pass(banks[("o0", half, b)], ("w", g, 0), E4M3, b, ("z", half, g), E5M2, first, last)
-
-        def store(engine, key):
-            result = outs.tile([P, N_TILE], F32, name="result")
-            src, dst = banks[key][:], result[:]
-            if key[0] == "o0":
-                src = src.rearrange("p (u m e) -> p m u e", u=2, e=2)
-                dst = dst.rearrange("p (m u e) -> p m u e", u=2, e=2)
-            if engine == "act":
-                nc.scalar.copy(out=dst, in_=src)
+        def store(engine, src, dst_view, result, hbm):
+            if engine == "scalar":
+                nc.scalar.copy(out=dst_view, in_=src)
             else:
-                nc.vector.tensor_copy(out=dst, in_=src)
-            view = out0_view if key[0] == "o0" else out1_view
-            nc.sync.dma_start(out=view[key[1], key[2]], in_=result[:])
+                nc.vector.tensor_copy(out=dst_view, in_=src)
+            nc.sync.dma_start(out=hbm, in_=result[:])
 
-        def out1_row(t):
-            for g in range(4):
-                mm_out1(t, g)
-                store("act", ("o1", t, g))
+        def out1_pass(bank, t, g, half):
+            mx_pass(bank, ("dz1", half, t), g, ("a", half), half == 0, half == HALVES - 1)
 
-        inter_w("act", 0)
-        dz_row(0, 0)
-        turn_dz(0, 0)
-        turned_out(("d", 0, 0))
-        inter_w("pool", 2)
-        inter_w("pool", 3)
-        inter_w("act", 1)
-        dz_row(0, 1)
-        turn_a(0)
-        turned_out(("a", 0, 0))
-        turn_dz(0, 1)
-        turned_out(("d", 0, 1))
-        spread_pa(2)
-        spread_pa(3)
-        dz_row(0, 2)
-        turn_a(1)
-        turned_out(("a", 1, 0))
-        turn_dz(0, 2)
-        turned_out(("d", 0, 2))
-        dz_row(0, 3)
-        inter_dz("pool", 0, 3)
-        inter_dz("act", 0, 0)
-        turn_dz(0, 3)
-        turned_out(("d", 0, 3))
-        dz_row(1, 0)
-        turn_dz(1, 0)
-        turned_out(("d", 1, 0))
-        inter_dz("act", 0, 1)
-        dz_row(1, 1)
-        turn_dz(1, 1)
-        turned_out(("d", 1, 1))
-        inter_dz("act", 0, 2)
+        def store_out1(bank, t, g):
+            result = outs.tile([P, BANK], F32, name="result")
+            store("scalar", bank[:], result[:], result, out1_view[t, g])
+
+        def out1_place(t):
+            for g in range(PASSES):
+                bank = psum.tile([P, BANK], F32, name="bank")
+                for half in range(HALVES):
+                    out1_pass(bank, t, g, half)
+                store_out1(bank, t, g)
+
+        out0_banks = {}
+
+        def out0_pass(half, g):
+            for b in range(I_TILES):
+                if g == 0:
+                    out0_banks[half, b] = psum.tile([P, BANK], F32, name="bank")
+                mx_pass(out0_banks[half, b], ("w", g), b, ("dz0", half, g), g == 0, g == PASSES - 1)
+
+        def store_out0(engine, half, b):
+            result = outs.tile([P, BANK], F32, name="result")
+            src = out0_banks[half, b][:].rearrange("p (u m e) -> p m u e", u=2, e=2)
+            dst = result[:].rearrange("p (m u e) -> p m u e", u=2, e=2)
+            store(engine, src, dst, result, out0_view[half, b])
+
+        interleave_w("scalar", 0)
+        for g in range(1, PASSES):
+            interleave_w("gpsimd", g)
+        for t in range(PLACES - 1):
+            dz_row(0, t)
+            if t < HALVES:
+                turn_a(t)
+            turn_dz(0, t)
+        dz_row(0, PLACES - 1)
+        interleave_dz("gpsimd", 0, 1)
+        interleave_dz("gpsimd", 0, 2)
+        interleave_dz("scalar", 0, 0)
+        turn_dz(0, PLACES - 1)
+        for t in range(2):
+            dz_row(1, t)
+            turn_dz(1, t)
+        interleave_dz("scalar", 0, 3)
         dz_row(1, 2)
         turn_dz(1, 2)
-        turned_out(("d", 1, 2))
-        quant(("d", 0, 0))
-        quant(("a", 0, 0))
-        quant(("d", 1, 0))
-        quant(("a", 1, 0))
-        out1_row(0)
-        quant(("d", 0, 1))
-        quant(("d", 1, 1))
-        out1_row(1)
+
+        place0 = []
+        for half in range(HALVES):
+            quantize(("dz1", half, 0))
+            quantize(("a", half))
+            for g in range(PASSES):
+                if half == 0:
+                    place0.append(psum.tile([P, BANK], F32, name="bank"))
+                out1_pass(place0[g], 0, g, half)
+        for g in range(PASSES):
+            store_out1(place0[g], 0, g)
+        for half in range(HALVES):
+            quantize(("dz1", half, 1))
+        out1_place(1)
         dz_row(1, 3)
         turn_dz(1, 3)
-        turned_out(("d", 1, 3))
-        quant(("d", 0, 2))
-        quant(("d", 1, 2))
-        out1_row(2)
-        inter_dz("act", 1, 3)
-        quant(("w", 0, 0))
-        quant(("z", 0, 0))
-        mm_out0(0, 0, True, False)
-        quant(("w", 1, 0))
-        quant(("z", 0, 1))
-        mm_out0(0, 1, False, False)
-        inter_dz("dve", 1, 0)
-        quant(("w", 2, 0))
-        quant(("z", 0, 2))
-        mm_out0(0, 2, False, False)
-        quant(("w", 3, 0))
-        quant(("z", 0, 3))
-        mm_out0(0, 3, False, True)
-        store("act", ("o0", 0, 0))
-        store("act", ("o0", 0, 1))
-        store("act", ("o0", 0, 2))
-        store("act", ("o0", 0, 3))
-        quant(("d", 0, 3))
-        quant(("d", 1, 3))
-        out1_row(3)
-        inter_dz("dve", 1, 1)
-        quant(("z", 1, 0))
-        mm_out0(1, 0, True, False)
-        quant(("z", 1, 3))
-        mm_out0(1, 3, False, False)
-        inter_dz("dve", 1, 2)
-        quant(("z", 1, 1))
-        mm_out0(1, 1, False, False)
-        quant(("z", 1, 2))
-        mm_out0(1, 2, False, True)
-        store("act", ("o0", 1, 0))
-        store("dve", ("o0", 1, 1))
-        store("act", ("o0", 1, 2))
-        store("dve", ("o0", 1, 3))
+
+        for half in range(HALVES):
+            quantize(("dz1", half, 2))
+        out1_place(2)
+        interleave_dz("scalar", 1, 1)
+        for g in range(PASSES):
+            if g == 2:
+                interleave_dz("vector", 1, 0)
+            quantize(("w", g))
+            quantize(("dz0", 0, g))
+            out0_pass(0, g)
+        for b in range(I_TILES):
+            store_out0("scalar", 0, b)
+        for half in range(HALVES):
+            quantize(("dz1", half, 3))
+        out1_place(3)
+        for g in range(PASSES):
+            if g % 2 == 0:
+                interleave_dz("vector", 1, 2 + g // 2)
+            quantize(("dz0", 1, g))
+            out0_pass(1, g)
+        for b in range(I_TILES):
+            store_out0("scalar" if b % 2 == 0 else "vector", 1, b)

from contextlib import ExitStack

import concourse.mybir as mybir
from concourse.masks import make_identity

F32 = mybir.dt.float32
BF16 = mybir.dt.bfloat16
U32 = mybir.dt.uint32
U8 = mybir.dt.uint8
E4M3 = mybir.dt.float8_e4m3fn_x4
E5M2 = mybir.dt.float8_e5m2_x4
ALU = mybir.AluOpType
ACT = mybir.ActivationFunctionType

CIN, COUT, V, S = 512, 128, 32, 16
EPS = 1e-5

P = 128
PLACES = 4
BANK = 512
PASSES = S * COUT // (P * PLACES)
HALVES = V * V // (P * PLACES)
S_PASS = S // PASSES
O_PARTS = P // S_PASS
HALF_V = V // HALVES
BANK_V = 8
PA_BANKS = V // BANK_V
PA_ROWS = S * PA_BANKS
I_TILES = CIN // P
RESULT_BUFS = 8

FLOPS = 2 * 2 * (S * COUT) * CIN * (V * V)
BYTES = 2 * (CIN * V * V + S * COUT * CIN + S * V * V + S * COUT * V + 2 * COUT + COUT * V) + 4 * (
    COUT * V + CIN * V * V + S * COUT * CIN
)


def tile_multiscale_gcn_pa_v_kernel(
    tc, ada_A, ada_w, ada_b, PA, feat, bn_gamma, bn_beta, bn_mean, bn_var, res, h, grad_out, out_0, out_1
):
    nc = tc.nc
    with ExitStack() as ctx:
        keep = ctx.enter_context(tc.tile_pool(name="keep", bufs=1))
        outs = ctx.enter_context(tc.tile_pool(name="outs", bufs=RESULT_BUFS))
        psum = ctx.enter_context(tc.psum_pool(name="psum", bufs=8))
        ctx.enter_context(tc.manual_schedule())

        var_sb = keep.tile([P, PLACES], BF16, name="var_sb")
        gamma_sb = keep.tile([P, PLACES], BF16, name="gamma_sb")
        h_sb = keep.tile([P, PLACES * V], F32, name="h_sb")
        grad_sb = keep.tile([P, PLACES * V], BF16, name="grad_sb")
        f_sb = keep.tile([P, PASSES * PLACES * V], BF16, name="f_sb")
        pa_sb = keep.tile([P, BANK_V * V], BF16, name="pa_sb")
        pa_sorted = keep.tile([P, P], F32, name="pa_sorted")
        f_sorted = keep.tile([P, PASSES * PLACES * V], BF16, name="f_sorted")
        w_sb = [keep.tile([P, PLACES * CIN], BF16, name="w_sb%d" % g) for g in range(PASSES)]
        a_sb = [keep.tile([P, I_TILES * BANK], BF16, name="a_sb%d" % half) for half in range(HALVES)]
        dz = [keep.tile([P, PLACES * PASSES * BANK], BF16, name="dz%d" % half) for half in range(HALVES)]
        ident = keep.tile([P, P], F32, name="ident")

        w_view = ada_w.rearrange("(g a) (c t) i -> g (a c) (t i)", a=S_PASS, t=PLACES)
        a_view = ada_A.rearrange("n (b p) (x v) w -> x p (n b) (v w)", p=P, x=HALVES)
        out0_view = out_0.rearrange("n (b p) (x v) w -> x (n b) p (v w)", p=P, x=HALVES)
        out1_view = out_1.rearrange("(g a) (c t) i -> t g (a c) i", a=S_PASS, t=PLACES)

        def per_channel(vec):
            return vec.rearrange("(c t) -> c t", t=PLACES).partition_broadcast(S_PASS)

        def per_channel_and_joint(x):
            return x.rearrange("n (c t) v x -> c (t v n x)", t=PLACES).partition_broadcast(S_PASS)

        nc.sync.dma_start(out=pa_sb[:PA_ROWS, :], in_=PA.rearrange("s (b v) w -> (s b) (v w)", b=PA_BANKS))
        nc.sync.dma_start(out=var_sb[:], in_=per_channel(bn_var))
        nc.sync.dma_start(out=h_sb[:], in_=per_channel_and_joint(h))
        nc.scalar.dma_start(
            out=f_sb[:].rearrange("p (g c) -> p g c", g=PASSES),
            in_=feat.rearrange("(g a) n (c t) w x -> (a c) g (t w n x)", a=S_PASS, t=PLACES),
        )
        nc.scalar.dma_start(out=grad_sb[:], in_=per_channel_and_joint(grad_out))
        nc.scalar.dma_start(out=gamma_sb[:], in_=per_channel(bn_gamma))
        make_identity(nc, ident[:])
        nc.vector.memset(pa_sorted[PA_ROWS:, :], 0.0)

        def load_w(g):
            nc.sync.dma_start(out=w_sb[g][:], in_=w_view[g])

        def load_a(half):
            nc.sync.dma_start(out=a_sb[half][:].rearrange("p (b c) -> p b c", b=I_TILES), in_=a_view[half])

        load_w(0)
        load_w(1)
        load_a(0)
        load_w(2)
        load_a(1)
        load_w(3)

        std = keep.tile([P, PLACES], F32, name="std")
        rstd = keep.tile([P, PLACES], F32, name="rstd")
        masked = keep.tile([P, PLACES * V], F32, name="masked")
        gained = keep.tile([P, PLACES * V], F32, name="gained")
        dy = keep.tile([P, PLACES * V], F32, name="dy")
        nc.scalar.activation(out=std[:], in_=var_sb[:], func=ACT.Sqrt, bias=EPS)

        nc.vector.tensor_copy(
            out=pa_sorted[:PA_ROWS, :].rearrange("p (v u c) -> p v u c", v=BANK_V, u=2),
            in_=pa_sb[:PA_ROWS, :].bitcast(F32).rearrange("p (v c u) -> p v u c", v=BANK_V, u=2),
        )
        pa_turned = psum.tile([P, BANK], F32, name="bank")
        nc.tensor.transpose(pa_turned[:, :P], pa_sorted[:], ident[:])
        pa_wide = []
        for b in range(PA_BANKS):
            wide = keep.tile([P, BANK], F32, name="pa_wide%d" % b)
            pa_wide.append(wide)
            s_part = S // 2 if b == 0 else S
            for s0 in range(0, S, s_part):
                columns = pa_turned[:, PA_BANKS * s0 + b : PA_BANKS * (s0 + s_part) : PA_BANKS]
                nc.scalar.copy(
                    out=wide[:].rearrange("p (s c) -> p s c", s=S)[:, s0 : s0 + s_part],
                    in_=columns.unsqueeze(2).to_broadcast([P, s_part, O_PARTS]),
                )
        pa_banks = []
        for b in range(PA_BANKS):
            pa_banks.append(psum.tile([P, BANK], F32, name="bank"))
            for g in range(PASSES):
                cols = slice(g * P, (g + 1) * P)
                nc.tensor.transpose(pa_banks[b][:, cols], pa_wide[b][:, cols], ident[:])

        def by_place(ap):
            return ap.rearrange("p (t v) -> p t v", t=PLACES)

        def over_joints(ap):
            return ap.unsqueeze(2).to_broadcast([P, PLACES, V])

        nc.vector.scalar_tensor_tensor(
            out=masked[:], in0=h_sb[:], scalar=0.0, in1=grad_sb[:], op0=ALU.is_gt, op1=ALU.mult
        )
        nc.vector.tensor_copy(
            out=f_sorted[:].bitcast(F32).rearrange("p (t g u c) -> p t g u c", t=PLACES, g=PASSES, u=2),
            in_=f_sb[:].bitcast(F32).rearrange("p (g t c u) -> p t g u c", t=PLACES, g=PASSES, u=2),
        )
        nc.vector.tensor_tensor(
            out=by_place(gained[:]), in0=by_place(masked[:]), in1=over_joints(gamma_sb[:]), op=ALU.mult
        )
        nc.vector.reciprocal(out=rstd[:], in_=std[:])
        nc.vector.tensor_tensor(out=by_place(dy[:]), in0=by_place(gained[:]), in1=over_joints(rstd[:]), op=ALU.mult)

        def dz_row(half, t):
            dz_view = dz[half][:].rearrange("p (t g u v c) -> p t v g u c", t=PLACES, g=PASSES, u=2, v=HALF_V)
            f_row = f_sorted[:, t * P : (t + 1) * P].rearrange("p (g u c) -> p g u c", g=PASSES, u=2)
            for v in range(HALF_V):
                joint = half * HALF_V + v
                pa_bank = pa_banks[joint // BANK_V][:].bitcast(BF16)
                pa_view = pa_bank.rearrange("p (g v u c) -> p v g u c", g=PASSES, v=BANK_V, u=2)
                nc.vector.scalar_tensor_tensor(
                    out=dz_view[:, t, v],
                    in0=f_row,
                    scalar=dy[:, t * V + joint : t * V + joint + 1],
                    in1=pa_view[:, joint % BANK_V],
                    op0=ALU.mult,
                    op1=ALU.mult,
                )

        grouped = {}
        codes = {}
        scales = {}

        def label(key):
            return "_".join(str(part) for part in key)

        def new_grouped(key):
            grouped[key] = keep.tile([P, BANK * PLACES], BF16, name="grouped_" + label(key), align_bytes=64)
            return grouped[key]

        def turn(key, block_words):
            turned = []
            for pair in range(2):
                bank = psum.tile([P, BANK], F32, name="bank")
                turned.append(bank)
                for j in range(2):
                    for u in range(2):
                        slot = (2 * j + u) * P
                        nc.tensor.transpose(bank[:, slot : slot + P], block_words(2 * pair + j, u), ident[:])
            dst = new_grouped(key)[:].bitcast(F32).rearrange("p (x j r u) -> p x j r u", x=2, j=2, u=2)
            for pair in range(2):
                src = turned[pair][:].rearrange("p (j u r) -> p j r u", j=2, u=2)
                nc.scalar.copy(out=dst[:, pair], in_=src)

        def turn_dz(half, t):
            words = dz[half][:].bitcast(F32)
            turn(("dz1", half, t), lambda g, u: words[:, ((t * PASSES + g) * 2 + u) * P :][:, :P])

        def turn_a(half):
            words = a_sb[half][:].bitcast(F32)
            turn(("a", half), lambda b, u: words[:, 2 * P * b + u : 2 * P * (b + 1) : 2])

        def interleave(engine, key, rows):
            tile = new_grouped(key)
            if engine == "gpsimd":
                for c0 in range(0, BANK, BANK // 2):
                    cols = slice(c0, c0 + BANK // 2)
                    nc.gpsimd.tensor_scalar(
                        out=tile[:].rearrange("p (c t) -> p c t", t=PLACES)[:, cols, :],
                        in0=rows.rearrange("p t c -> p c t")[:, cols, :],
                        scalar1=1.0,
                        scalar2=0.0,
                        op0=ALU.mult,
                        op1=ALU.add,
                    )
                return
            dst = tile[:].rearrange("p (c i t) -> p c t i", i=4, t=PLACES)
            src = rows.rearrange("p t (c i) -> p c t i", i=4)
            if engine == "scalar":
                nc.scalar.copy(out=dst, in_=src)
            else:
                nc.vector.tensor_copy(out=dst, in_=src)

        def interleave_w(engine, g):
            interleave(engine, ("w", g), w_sb[g][:].rearrange("p (t c) -> p t c", t=PLACES))

        def interleave_dz(engine, half, g):
            rows = dz[half][:].rearrange("p (t g c) -> p g t c", t=PLACES, g=PASSES)[:, g]
            interleave(engine, ("dz0", half, g), rows)

        def fmt(key):
            return E4M3 if key[0] in ("w", "a") else E5M2

        def quantize(key):
            codes[key] = keep.tile([P, BANK], U32, name="codes_" + label(key), align_bytes=64)
            scales[key] = keep.tile([P, BANK], U8, name="scales_" + label(key), align_bytes=64)
            nc.vector.quantize_mx(out=codes[key][:].bitcast(fmt(key)), scales=scales[key][:], in_=grouped[key][:])

        def mx_pass(bank, stationary, j, moving, start, stop):
            cols = slice(j * P, (j + 1) * P)
            nc.tensor.matmul_mx(
                out=bank[:],
                lhsT=codes[stationary][:, cols].bitcast(fmt(stationary)),
                lhsT_scale=scales[stationary][:, cols],
                rhs=codes[moving][:].bitcast(fmt(moving)),
                rhs_scale=scales[moving][:],
                start=start,
                stop=stop,
            )

        def store(engine, src, dst_view, result, hbm):
            if engine == "scalar":
                nc.scalar.copy(out=dst_view, in_=src)
            else:
                nc.vector.tensor_copy(out=dst_view, in_=src)
            nc.sync.dma_start(out=hbm, in_=result[:])

        def out1_pass(bank, t, g, half):
            mx_pass(bank, ("dz1", half, t), g, ("a", half), half == 0, half == HALVES - 1)

        def store_out1(bank, t, g):
            result = outs.tile([P, BANK], F32, name="result")
            store("scalar", bank[:], result[:], result, out1_view[t, g])

        def out1_place(t):
            for g in range(PASSES):
                bank = psum.tile([P, BANK], F32, name="bank")
                for half in range(HALVES):
                    out1_pass(bank, t, g, half)
                store_out1(bank, t, g)

        out0_banks = {}

        def out0_pass(half, g):
            for b in range(I_TILES):
                if g == 0:
                    out0_banks[half, b] = psum.tile([P, BANK], F32, name="bank")
                mx_pass(out0_banks[half, b], ("w", g), b, ("dz0", half, g), g == 0, g == PASSES - 1)

        def store_out0(engine, half, b):
            result = outs.tile([P, BANK], F32, name="result")
            src = out0_banks[half, b][:].rearrange("p (u m e) -> p m u e", u=2, e=2)
            dst = result[:].rearrange("p (m u e) -> p m u e", u=2, e=2)
            store(engine, src, dst, result, out0_view[half, b])

        interleave_w("scalar", 0)
        for g in range(1, PASSES):
            interleave_w("gpsimd", g)
        for t in range(PLACES - 1):
            dz_row(0, t)
            if t < HALVES:
                turn_a(t)
            turn_dz(0, t)
        dz_row(0, PLACES - 1)
        interleave_dz("gpsimd", 0, 1)
        interleave_dz("gpsimd", 0, 2)
        interleave_dz("scalar", 0, 0)
        turn_dz(0, PLACES - 1)
        for t in range(2):
            dz_row(1, t)
            turn_dz(1, t)
        interleave_dz("scalar", 0, 3)
        dz_row(1, 2)
        turn_dz(1, 2)

        place0 = []
        for half in range(HALVES):
            quantize(("dz1", half, 0))
            quantize(("a", half))
            for g in range(PASSES):
                if half == 0:
                    place0.append(psum.tile([P, BANK], F32, name="bank"))
                out1_pass(place0[g], 0, g, half)
        for g in range(PASSES):
            store_out1(place0[g], 0, g)
        for half in range(HALVES):
            quantize(("dz1", half, 1))
        out1_place(1)
        dz_row(1, 3)
        turn_dz(1, 3)

        for half in range(HALVES):
            quantize(("dz1", half, 2))
        out1_place(2)
        interleave_dz("scalar", 1, 1)
        for g in range(PASSES):
            if g == 2:
                interleave_dz("vector", 1, 0)
            quantize(("w", g))
            quantize(("dz0", 0, g))
            out0_pass(0, g)
        for b in range(I_TILES):
            store_out0("scalar", 0, b)
        for half in range(HALVES):
            quantize(("dz1", half, 3))
        out1_place(3)
        for g in range(PASSES):
            if g % 2 == 0:
                interleave_dz("vector", 1, 2 + g // 2)
            quantize(("dz0", 1, g))
            out0_pass(1, g)
        for b in range(I_TILES):
            store_out0("scalar" if b % 2 == 0 else "vector", 1, b)
